import numpy as np
import ml_dtypes

BF16 = ml_dtypes.bfloat16


def bf(x):
    return np.asarray(x, np.float32).astype(BF16)


def f32(x):
    return np.asarray(x, np.float32)


def f64(x):
    return np.asarray(x).astype(np.float64)


def striped(idx):
    return np.tile(idx.reshape(-1, 16).T, (8, 1))


C, S, N = 128, 2048, 512


def setup_inputs():
    z = np.random.standard_normal((C, N)) * np.random.uniform(0.15, 0.45, (1, N))
    return {"base": f32(np.random.standard_normal((C, S)) / np.sqrt(C)), "z": f32(z), "offs": striped(np.random.permutation(S)[:N])}


def reference(base, z, offs):
    idx = offs[:16].T.reshape(-1)
    zz = f64(z)
    rn = 1.0 / np.sqrt((zz * zz).sum(axis=0, keepdims=True))
    out = f64(base).copy()
    out[:, idx] = zz * rn
    return out

@@ -1,0 +1,37 @@
+import concourse.mybir as mybir
+
+C, S, N = 128, 2048, 512
+F32, BF16, U16 = mybir.dt.float32, mybir.dt.bfloat16, mybir.dt.uint16
+MULT = mybir.AluOpType.mult
+SQRT = mybir.ActivationFunctionType.Sqrt
+
+FLOPS = 3 * C * N
+
+
+def tile_relationaltemporalcontrastiveloss_kernel(tc, base, z, offs, out):
+    nc = tc.nc
+    with (
+        tc.tile_pool(name="held", bufs=1) as held,
+        tc.psum_pool(name="psum", bufs=1) as psum,
+    ):
+        offsets = held.tile([C, N // 16], U16, name="offsets")
+        nc.sync.dma_start(offsets[:], offs)
+        z_sb = held.tile([C, N], F32, name="z_sb")
+        nc.sync.dma_start(z_sb[:], z)
+        bank = held.tile([C, S], F32, name="bank")
+        nc.scalar.dma_start(bank[:], base)
+
+        ones = held.tile([C, C], BF16, name="ones")
+        nc.vector.memset(ones[:], 1.0)
+        squares = held.tile([C, N], BF16, name="squares")
+        nc.vector.tensor_tensor(squares[:], z_sb[:], z_sb[:], MULT)
+        sums = psum.tile([C, N], F32, name="sums")
+        nc.tensor.matmul(sums[:], ones[:], squares[:], start=True, stop=True)
+
+        lengths = held.tile([C, N], F32, name="lengths")
+        nc.scalar.activation(lengths[:], sums[:], SQRT)
+        rn = held.tile([C, N], F32, name="rn")
+        nc.vector.reciprocal(rn[:], lengths[:])
+
+        nc.vector.tensor_tensor(bank[:].indirect(offsets[:]), z_sb[:], rn[:], MULT)
+        nc.sync.dma_start(out, bank[:])

@@ -3,7 +3,7 @@ import concourse.mybir as mybir
 C, S, N = 128, 2048, 512
 F32, BF16, U16 = mybir.dt.float32, mybir.dt.bfloat16, mybir.dt.uint16
 MULT = mybir.AluOpType.mult
-SQRT = mybir.ActivationFunctionType.Sqrt
+RSQRT = mybir.ActivationFunctionType.Abs_reciprocal_sqrt
 
 FLOPS = 3 * C * N
 
@@ -28,10 +28,8 @@ def tile_relationaltemporalcontrastiveloss_kernel(tc, base, z, offs, out):
         sums = psum.tile([C, N], F32, name="sums")
         nc.tensor.matmul(sums[:], ones[:], squares[:], start=True, stop=True)
 
-        lengths = held.tile([C, N], F32, name="lengths")
-        nc.scalar.activation(lengths[:], sums[:], SQRT)
         rn = held.tile([C, N], F32, name="rn")
-        nc.vector.reciprocal(rn[:], lengths[:])
+        nc.scalar.activation(rn[:], sums[:], RSQRT)
 
         nc.vector.tensor_tensor(bank[:].indirect(offsets[:]), z_sb[:], rn[:], MULT)
         nc.sync.dma_start(out, bank[:])

@@ -3,6 +3,7 @@ import concourse.mybir as mybir
 C, S, N = 128, 2048, 512
 F32, BF16, U16 = mybir.dt.float32, mybir.dt.bfloat16, mybir.dt.uint16
 MULT = mybir.AluOpType.mult
+SQUARE = mybir.ActivationFunctionType.Square
 RSQRT = mybir.ActivationFunctionType.Abs_reciprocal_sqrt
 
 FLOPS = 3 * C * N
@@ -10,26 +11,33 @@ FLOPS = 3 * C * N
 
 def tile_relationaltemporalcontrastiveloss_kernel(tc, base, z, offs, out):
     nc = tc.nc
+    half_n, half_s = N // 2, S // 2
     with (
         tc.tile_pool(name="held", bufs=1) as held,
         tc.psum_pool(name="psum", bufs=1) as psum,
     ):
-        offsets = held.tile([C, N // 16], U16, name="offsets")
-        nc.sync.dma_start(offsets[:], offs)
         z_sb = held.tile([C, N], F32, name="z_sb")
-        nc.sync.dma_start(z_sb[:], z)
+        offsets = held.tile([C, N // 16], U16, name="offsets")
         bank = held.tile([C, S], F32, name="bank")
-        nc.scalar.dma_start(bank[:], base)
+        nc.sync.dma_start(z_sb[:, :half_n], z[:, :half_n])
+        nc.scalar.dma_start(z_sb[:, half_n:], z[:, half_n:])
+        nc.sync.dma_start(offsets[:], offs)
+        nc.sync.dma_start(bank[:, :half_s], base[:, :half_s])
+        nc.scalar.dma_start(bank[:, half_s:], base[:, half_s:])
 
         ones = held.tile([C, C], BF16, name="ones")
         nc.vector.memset(ones[:], 1.0)
-        squares = held.tile([C, N], BF16, name="squares")
-        nc.vector.tensor_tensor(squares[:], z_sb[:], z_sb[:], MULT)
-        sums = psum.tile([C, N], F32, name="sums")
-        nc.tensor.matmul(sums[:], ones[:], squares[:], start=True, stop=True)
 
+        squares = held.tile([C, N], BF16, name="squares")
+        nc.scalar.activation(squares[:, :half_n], z_sb[:, :half_n], SQUARE)
+        nc.vector.tensor_tensor(squares[:, half_n:], z_sb[:, half_n:], z_sb[:, half_n:], MULT)
         rn = held.tile([C, N], F32, name="rn")
-        nc.scalar.activation(rn[:], sums[:], RSQRT)
+        for h in range(2):
+            cols = slice(h * half_n, (h + 1) * half_n)
+            sums = psum.tile([C, half_n], F32, name=f"sums{h}")
+            nc.tensor.matmul(sums[:], ones[:], squares[:, cols], start=True, stop=True)
+            nc.scalar.activation(rn[:, cols], sums[:], RSQRT)
 
         nc.vector.tensor_tensor(bank[:].indirect(offsets[:]), z_sb[:], rn[:], MULT)
-        nc.sync.dma_start(out, bank[:])
+        nc.sync.dma_start(out[:, :half_s], bank[:, :half_s])
+        nc.scalar.dma_start(out[:, half_s:], bank[:, half_s:])

@@ -39,5 +39,4 @@ def tile_relationaltemporalcontrastiveloss_kernel(tc, base, z, offs, out):
             nc.scalar.activation(rn[:, cols], sums[:], RSQRT)
 
         nc.vector.tensor_tensor(bank[:].indirect(offsets[:]), z_sb[:], rn[:], MULT)
-        nc.sync.dma_start(out[:, :half_s], bank[:, :half_s])
-        nc.scalar.dma_start(out[:, half_s:], bank[:, half_s:])
+        nc.sync.dma_start(out, bank[:])

@@ -6,6 +6,7 @@ MULT = mybir.AluOpType.mult
 SQUARE = mybir.ActivationFunctionType.Square
 RSQRT = mybir.ActivationFunctionType.Abs_reciprocal_sqrt
 
+WARM_MATMULS = 12
 FLOPS = 3 * C * N
 
 
@@ -28,6 +29,10 @@ def tile_relationaltemporalcontrastiveloss_kernel(tc, base, z, offs, out):
         ones = held.tile([C, C], BF16, name="ones")
         nc.vector.memset(ones[:], 1.0)
 
+        warm = psum.tile([C, C], F32, name="warm")
+        for w in range(WARM_MATMULS):
+            nc.tensor.matmul(warm[:], ones[:], ones[:], start=True, stop=True)
+
         squares = held.tile([C, N], BF16, name="squares")
         nc.scalar.activation(squares[:, :half_n], z_sb[:, :half_n], SQUARE)
         nc.vector.tensor_tensor(squares[:, half_n:], z_sb[:, half_n:], z_sb[:, half_n:], MULT)
@@ -39,4 +44,5 @@ def tile_relationaltemporalcontrastiveloss_kernel(tc, base, z, offs, out):
             nc.scalar.activation(rn[:, cols], sums[:], RSQRT)
 
         nc.vector.tensor_tensor(bank[:].indirect(offsets[:]), z_sb[:], rn[:], MULT)
-        nc.sync.dma_start(out, bank[:])
+        nc.sync.dma_start(out[:, :half_s], bank[:, :half_s])
+        nc.scalar.dma_start(out[:, half_s:], bank[:, half_s:])

@@ -3,10 +3,8 @@ import concourse.mybir as mybir
 C, S, N = 128, 2048, 512
 F32, BF16, U16 = mybir.dt.float32, mybir.dt.bfloat16, mybir.dt.uint16
 MULT = mybir.AluOpType.mult
-SQUARE = mybir.ActivationFunctionType.Square
 RSQRT = mybir.ActivationFunctionType.Abs_reciprocal_sqrt
 
-WARM_MATMULS = 12
 FLOPS = 3 * C * N
 
 
@@ -29,20 +27,14 @@ def tile_relationaltemporalcontrastiveloss_kernel(tc, base, z, offs, out):
         ones = held.tile([C, C], BF16, name="ones")
         nc.vector.memset(ones[:], 1.0)
 
-        warm = psum.tile([C, C], F32, name="warm")
-        for w in range(WARM_MATMULS):
-            nc.tensor.matmul(warm[:], ones[:], ones[:], start=True, stop=True)
-
         squares = held.tile([C, N], BF16, name="squares")
-        nc.scalar.activation(squares[:, :half_n], z_sb[:, :half_n], SQUARE)
-        nc.vector.tensor_tensor(squares[:, half_n:], z_sb[:, half_n:], z_sb[:, half_n:], MULT)
         rn = held.tile([C, N], F32, name="rn")
         for h in range(2):
             cols = slice(h * half_n, (h + 1) * half_n)
+            nc.vector.tensor_tensor(squares[:, cols], z_sb[:, cols], z_sb[:, cols], MULT)
             sums = psum.tile([C, half_n], F32, name=f"sums{h}")
             nc.tensor.matmul(sums[:], ones[:], squares[:, cols], start=True, stop=True)
             nc.scalar.activation(rn[:, cols], sums[:], RSQRT)
 
         nc.vector.tensor_tensor(bank[:].indirect(offsets[:]), z_sb[:], rn[:], MULT)
-        nc.sync.dma_start(out[:, :half_s], bank[:, :half_s])
-        nc.scalar.dma_start(out[:, half_s:], bank[:, half_s:])
+        nc.sync.dma_start(out, bank[:])

@@ -10,7 +10,7 @@ FLOPS = 3 * C * N
 
 def tile_relationaltemporalcontrastiveloss_kernel(tc, base, z, offs, out):
     nc = tc.nc
-    half_n, half_s = N // 2, S // 2
+    half_n = N // 2
     with (
         tc.tile_pool(name="held", bufs=1) as held,
         tc.psum_pool(name="psum", bufs=1) as psum,
@@ -18,11 +18,9 @@ def tile_relationaltemporalcontrastiveloss_kernel(tc, base, z, offs, out):
         z_sb = held.tile([C, N], F32, name="z_sb")
         offsets = held.tile([C, N // 16], U16, name="offsets")
         bank = held.tile([C, S], F32, name="bank")
-        nc.sync.dma_start(z_sb[:, :half_n], z[:, :half_n])
-        nc.scalar.dma_start(z_sb[:, half_n:], z[:, half_n:])
+        nc.sync.dma_start(z_sb[:], z)
         nc.sync.dma_start(offsets[:], offs)
-        nc.sync.dma_start(bank[:, :half_s], base[:, :half_s])
-        nc.scalar.dma_start(bank[:, half_s:], base[:, half_s:])
+        nc.sync.dma_start(bank[:], base)
 
         ones = held.tile([C, C], BF16, name="ones")
         nc.vector.memset(ones[:], 1.0)

@@ -10,7 +10,6 @@ FLOPS = 3 * C * N
 
 def tile_relationaltemporalcontrastiveloss_kernel(tc, base, z, offs, out):
     nc = tc.nc
-    half_n = N // 2
     with (
         tc.tile_pool(name="held", bufs=1) as held,
         tc.psum_pool(name="psum", bufs=1) as psum,
@@ -26,13 +25,11 @@ def tile_relationaltemporalcontrastiveloss_kernel(tc, base, z, offs, out):
         nc.vector.memset(ones[:], 1.0)
 
         squares = held.tile([C, N], BF16, name="squares")
+        nc.vector.tensor_tensor(squares[:], z_sb[:], z_sb[:], MULT)
+        sums = psum.tile([C, N], F32, name="sums")
+        nc.tensor.matmul(sums[:], ones[:], squares[:], start=True, stop=True)
         rn = held.tile([C, N], F32, name="rn")
-        for h in range(2):
-            cols = slice(h * half_n, (h + 1) * half_n)
-            nc.vector.tensor_tensor(squares[:, cols], z_sb[:, cols], z_sb[:, cols], MULT)
-            sums = psum.tile([C, half_n], F32, name=f"sums{h}")
-            nc.tensor.matmul(sums[:], ones[:], squares[:, cols], start=True, stop=True)
-            nc.scalar.activation(rn[:, cols], sums[:], RSQRT)
+        nc.scalar.activation(rn[:], sums[:], RSQRT)
 
         nc.vector.tensor_tensor(bank[:].indirect(offsets[:]), z_sb[:], rn[:], MULT)
         nc.sync.dma_start(out, bank[:])

@@ -14,9 +14,9 @@ def tile_relationaltemporalcontrastiveloss_kernel(tc, base, z, offs, out):
         tc.tile_pool(name="held", bufs=1) as held,
         tc.psum_pool(name="psum", bufs=1) as psum,
     ):
-        z_sb = held.tile([C, N], F32, name="z_sb")
+        bank = held.tile([C, S], F32, name="bank", align_bytes=256)
+        z_sb = held.tile([C, N], F32, name="z_sb", align_bytes=256)
         offsets = held.tile([C, N // 16], U16, name="offsets")
-        bank = held.tile([C, S], F32, name="bank")
         nc.sync.dma_start(z_sb[:], z)
         nc.sync.dma_start(offsets[:], offs)
         nc.sync.dma_start(bank[:], base)

@@ -10,6 +10,7 @@ FLOPS = 3 * C * N
 
 def tile_relationaltemporalcontrastiveloss_kernel(tc, base, z, offs, out):
     nc = tc.nc
+    half_n = N // 2
     with (
         tc.tile_pool(name="held", bufs=1) as held,
         tc.psum_pool(name="psum", bufs=1) as psum,
@@ -25,11 +26,13 @@ def tile_relationaltemporalcontrastiveloss_kernel(tc, base, z, offs, out):
         nc.vector.memset(ones[:], 1.0)
 
         squares = held.tile([C, N], BF16, name="squares")
-        nc.vector.tensor_tensor(squares[:], z_sb[:], z_sb[:], MULT)
-        sums = psum.tile([C, N], F32, name="sums")
-        nc.tensor.matmul(sums[:], ones[:], squares[:], start=True, stop=True)
         rn = held.tile([C, N], F32, name="rn")
-        nc.scalar.activation(rn[:], sums[:], RSQRT)
+        for h in range(2):
+            cols = slice(h * half_n, (h + 1) * half_n)
+            nc.vector.tensor_tensor(squares[:, cols], z_sb[:, cols], z_sb[:, cols], MULT)
+            sums = psum.tile([C, half_n], F32, name=f"sums{h}")
+            nc.tensor.matmul(sums[:], ones[:], squares[:, cols], start=True, stop=True)
+            nc.scalar.activation(rn[:, cols], sums[:], RSQRT)
 
         nc.vector.tensor_tensor(bank[:].indirect(offsets[:]), z_sb[:], rn[:], MULT)
         nc.sync.dma_start(out, bank[:])

@@ -20,7 +20,8 @@ def tile_relationaltemporalcontrastiveloss_kernel(tc, base, z, offs, out):
         offsets = held.tile([C, N // 16], U16, name="offsets")
         nc.sync.dma_start(z_sb[:], z)
         nc.sync.dma_start(offsets[:], offs)
-        nc.sync.dma_start(bank[:], base)
+        nc.sync.dma_start(bank[:, : S // 2], base[:, : S // 2])
+        nc.scalar.dma_start(bank[:, S // 2 :], base[:, S // 2 :])
 
         ones = held.tile([C, C], BF16, name="ones")
         nc.vector.memset(ones[:], 1.0)

import concourse.mybir as mybir

C, S, N = 128, 2048, 512
F32, BF16, U16 = mybir.dt.float32, mybir.dt.bfloat16, mybir.dt.uint16
MULT = mybir.AluOpType.mult
RSQRT = mybir.ActivationFunctionType.Abs_reciprocal_sqrt

FLOPS = 3 * C * N


def tile_relationaltemporalcontrastiveloss_kernel(tc, base, z, offs, out):
    nc = tc.nc
    half_n = N // 2
    with (
        tc.tile_pool(name="held", bufs=1) as held,
        tc.psum_pool(name="psum", bufs=1) as psum,
    ):
        bank = held.tile([C, S], F32, name="bank", align_bytes=256)
        z_sb = held.tile([C, N], F32, name="z_sb", align_bytes=256)
        offsets = held.tile([C, N // 16], U16, name="offsets")
        nc.sync.dma_start(z_sb[:], z)
        nc.sync.dma_start(offsets[:], offs)
        nc.sync.dma_start(bank[:, : S // 2], base[:, : S // 2])
        nc.scalar.dma_start(bank[:, S // 2 :], base[:, S // 2 :])

        ones = held.tile([C, C], BF16, name="ones")
        nc.vector.memset(ones[:], 1.0)

        squares = held.tile([C, N], BF16, name="squares")
        rn = held.tile([C, N], F32, name="rn")
        for h in range(2):
            cols = slice(h * half_n, (h + 1) * half_n)
            nc.vector.tensor_tensor(squares[:, cols], z_sb[:, cols], z_sb[:, cols], MULT)
            sums = psum.tile([C, half_n], F32, name=f"sums{h}")
            nc.tensor.matmul(sums[:], ones[:], squares[:, cols], start=True, stop=True)
            nc.scalar.activation(rn[:, cols], sums[:], RSQRT)

        nc.vector.tensor_tensor(bank[:].indirect(offsets[:]), z_sb[:], rn[:], MULT)
        nc.sync.dma_start(out, bank[:])
